import numpy as np
import ml_dtypes


def mxq(x, axis, fmt="e4m3"):
    dtype, down = {"e4m3": (ml_dtypes.float8_e4m3fn, 7), "e5m2": (ml_dtypes.float8_e5m2, 14)}[fmt]
    v = np.moveaxis(np.asarray(x, np.float32).astype(ml_dtypes.bfloat16).astype(np.float64), axis, -1)
    blocks = v.reshape(v.shape[:-1] + (-1, 32))
    amax = np.abs(blocks).max(-1, keepdims=True)
    byte = np.maximum(np.where(amax > 0, np.frexp(amax)[1] - 1 + 127, 0) - down, 1)
    scale = np.exp2(byte - 127.0)
    codes = (blocks / scale).astype(np.float32).astype(dtype).astype(np.float64)
    return np.moveaxis((codes * scale).reshape(v.shape), -1, axis)


WIDE = False


def mx_kscale(k):
    if not WIDE:
        return np.ones(k)
    levels = np.array([10, -10, 5, -5, 0])
    if k % 512:
        return np.exp2(np.random.permutation(np.resize(levels, k // 32))).repeat(32)
    a = np.empty((k // 512, 16))
    for p in range(k // 512):
        a[p, :8] = np.random.permutation(np.resize(levels, 8))
        for g in range(8):
            far = levels[np.abs(levels - a[p, g]) >= 10]
            a[p, g + 8] = far[np.random.randint(len(far))]
    return np.exp2(a.ravel()).repeat(32)


BF16 = ml_dtypes.bfloat16


def bf(x):
    return np.asarray(x, np.float32).astype(BF16)


def f64(x):
    return np.asarray(x).astype(np.float64)


E2M1 = np.array([0.0, 0.5, 1.0, 1.5, 2.0, 3.0, 4.0, 6.0, -0.0, -0.5, -1.0, -1.5, -2.0, -3.0, -4.0, -6.0])


def pack_weight(w, fmt):
    k, n = w.shape
    w = f64(bf(w)).reshape(k // 32, 32, n)
    amax = np.abs(w).max(1)
    if fmt == "e4m3":
        byte = np.frexp(amax)[1] - 1 + 127 - 7
    else:
        mant, ex = np.frexp(amax / 6.0)
        byte = np.where(mant > 0.5, ex, ex - 1) + 127
    byte = np.clip(np.where(amax > 0, byte, 1), 1, 254)
    scaled = (w * np.exp2(127.0 - byte)[:, None, :]).reshape(k, n).astype(np.float32)
    by_word = np.ascontiguousarray(scaled.reshape(k // 512, 128, 4, n).transpose(0, 1, 3, 2))
    if fmt == "e4m3":
        words = by_word.astype(ml_dtypes.float8_e4m3fn).view(np.uint8)
    else:
        c = by_word.astype(ml_dtypes.float4_e2m1fn).view(np.uint8) & 0xF
        words = c[..., 0::2] | (c[..., 1::2] << 4)
    return np.ascontiguousarray(words), np.ascontiguousarray(byte.astype(np.uint8).reshape(k // 512, 16, n))


def unpack_weight(words, scales, fmt):
    g, p, n, _ = words.shape
    if fmt == "e4m3":
        vals = np.ascontiguousarray(words).view(ml_dtypes.float8_e4m3fn).astype(np.float64)
    else:
        nib = np.empty((g, p, n, 4), np.uint8)
        nib[..., 0::2] = words & 0xF
        nib[..., 1::2] = words >> 4
        vals = E2M1[nib]
    vals = vals * np.repeat(np.exp2(scales.astype(np.float64) - 127.0), 8, axis=1)[..., None]
    return vals.transpose(0, 1, 3, 2).reshape(g * 512, n)
def pack4(w):
    words, scales = pack_weight(w, "e2m1")
    return words.reshape(words.shape[0], 128, -1), scales


def unpack4(words, scales):
    return unpack_weight(words.reshape(words.shape[0], 128, -1, 2), scales, "e2m1")


B, CL, CH, CK, CV, CO, H, W = 2, 1024, 2048, 256, 512, 1024, 24, 24
N = H * W
CF = CO + CH
EPS = 1e-5


def draw0():
    s = mx_kscale(CV)
    t = mx_kscale(CF)
    tc, th = t[:CO], t[CO:]
    context = bf(np.random.standard_normal((B, CV, H, W)) * 0.4 * s[None, :, None, None])
    high_feats = bf(np.random.standard_normal((B, CH, H, W)) * th[None, :, None, None])
    ww = np.random.standard_normal((CO, CV)) * 2.0 / np.sqrt(CV) / s[None, :] * tc[:, None]
    ww_words, ww_scales = pack4(ww.T)
    bw = bf(np.random.standard_normal(CO) * 0.3 * tc)
    wf = np.random.standard_normal((CO, CF)) / np.sqrt(CF) / t[None, :]
    wf_words, wf_scales = pack4(wf.T)
    return {"context": context,
            "high_feats": high_feats,
            "ww_words": ww_words,
            "ww_scales": ww_scales,
            "bw": bw,
            "wf_words": wf_words,
            "wf_scales": wf_scales,
            "bfuse": bf(np.random.standard_normal(CO) * 0.3),
            "gf": bf(np.random.uniform(0.5, 1.5, CO)),
            "bef": bf(np.random.standard_normal(CO) * 0.3),
            "mf": bf(np.random.standard_normal(CO) * 0.3),
            "vf": bf(np.random.uniform(0.5, 1.5, CO))}


def core(context, high_feats, ww_words, ww_scales, bw, wf_words, wf_scales, bfuse, gf, bef, mf, vf):
    ctx = f64(context).reshape(B, CV, N)
    hi = f64(high_feats).reshape(B, CH, N)
    c = (unpack4(ww_words, ww_scales).T @ mxq(ctx, 1, "e4m3")) + f64(bw)[None, :, None]
    fused = np.concatenate([c, hi], axis=1)
    y = (unpack4(wf_words, wf_scales).T @ mxq(fused, 1, "e4m3")) + f64(bfuse)[None, :, None]
    sc = f64(gf) / np.sqrt(f64(vf) + EPS)
    out = (y - f64(mf)[None, :, None]) * sc[None, :, None] + f64(bef)[None, :, None]
    return out.reshape(B, CO, H, W)


def e4m3fn_bytes(y):
    return np.clip(np.asarray(y, np.float64), -448.0, 448.0).astype(np.float32).astype(ml_dtypes.float8_e4m3fn).view(np.uint8)


def e4m3fn_values(b):
    return np.asarray(b, np.uint8).view(ml_dtypes.float8_e4m3fn).astype(np.float64)


def setup_inputs():
    d = draw0()
    x0 = np.asarray(d['high_feats']).astype(np.float64)
    s = (np.max(np.abs(x0), axis=(0, 2, 3), keepdims=True) / 448.0).astype(np.float32)
    out = {}
    for k, v in d.items():
        if k == 'high_feats':
            out['high_feats_bytes'] = e4m3fn_bytes(x0 / s.astype(np.float64))
            out['high_feats_scale'] = s
        else:
            out[k] = v
    return out


def reference(context, high_feats_bytes, high_feats_scale, ww_words, ww_scales, bw, wf_words, wf_scales, bfuse, gf, bef, mf, vf):
    return core(context, e4m3fn_values(high_feats_bytes) * high_feats_scale.astype(np.float64), ww_words, ww_scales, bw, wf_words, wf_scales, bfuse, gf, bef, mf, vf)

@@ -1,0 +1,413 @@
+from contextlib import ExitStack
+
+import concourse.mybir as mybir
+from concourse.masks import make_identity
+
+B, CV, CH, CO, NPIX = 2, 512, 2048, 1024, 576
+CF = CO + CH
+EPS = 1e-5
+FLOPS = 2 * B * NPIX * CO * (CV + CF)
+
+F32 = mybir.dt.float32
+BF16 = mybir.dt.bfloat16
+U32 = mybir.dt.uint32
+I32 = mybir.dt.int32
+U8 = mybir.dt.uint8
+FP8 = mybir.dt.float8_e4m3fn
+FP8X4 = mybir.dt.float8_e4m3fn_x4
+FP4X4 = mybir.dt.float4_e2m1fn_x4
+ADD = mybir.AluOpType.add
+SUB = mybir.AluOpType.subtract
+MULT = mybir.AluOpType.mult
+POW = mybir.AluOpType.pow
+IDENT = mybir.ActivationFunctionType.Identity
+COPY = mybir.ActivationFunctionType.Copy
+
+P = 128
+PACK = 4
+KG = CF // 512
+HG = CH // 512
+MT = CO // P
+SHARE = (256, 64)
+
+
+def tile_afnb_pb_w4_kernel(
+    tc, context, high_feats_bytes, high_feats_scale, ww_words, ww_scales, bw, wf_words, wf_scales, bfuse, gf, bef, mf, vf, out
+):
+    nc = tc.nc
+    with ExitStack() as ctx:
+        keep = ctx.enter_context(tc.tile_pool(name="keep", bufs=1))
+        wide_pool = ctx.enter_context(tc.tile_pool(name="wide", bufs=4))
+        inter_pool = ctx.enter_context(tc.tile_pool(name="inter", bufs=3))
+        y_pool = ctx.enter_context(tc.tile_pool(name="y", bufs=8))
+        psum = ctx.enter_context(tc.psum_pool(name="psum", bufs=1))
+        ctx.enter_context(tc.manual_schedule())
+
+        def sb(name, shape, dt):
+            return keep.tile(shape, dt, name=name, align_bytes=64)
+
+        def bank(i, shape, dt=F32):
+            return psum.tile(shape, dt, name="bank%d" % i)
+
+        NALL = B * NPIX
+        ctx_raw = [sb("ctx_raw%d" % b, [P, PACK, NPIX], BF16) for b in range(B)]
+        ctx_int = [sb("ctx_int%d" % b, [P, NPIX, PACK], BF16) for b in range(B)]
+        ctx_q = sb("ctx_q", [P, NALL], U32)
+        ctx_s = sb("ctx_s", [P, NALL], U8)
+        hi_raw = [[sb("hi_raw%d_%d" % (b, g), [P, PACK, NPIX], U8) for g in range(HG)] for b in range(B)]
+        c_int = [sb("c_int%d" % h, [P, NALL, PACK], BF16) for h in range(2)]
+        kq = [sb("kq%d" % g, [P, NALL], U32) for g in range(KG)]
+        ks = [sb("ks%d" % g, [P, NALL], U8) for g in range(KG)]
+        ww_raw = sb("ww_raw", [P, 2 * CO], U8)
+        ww_q = sb("ww_q", [P, 2 * CO], U8)
+        ww_sraw = sb("ww_sraw", [P, CO], U8)
+        ww_s = sb("ww_s", [P, CO], U8)
+        wf_q = [sb("wf_q%d" % g, [P, 2 * CO], U8) for g in range(KG)]
+        wf_s = sb("wf_s", [P, KG, CO], U8)
+        hs = sb("hs", [P, HG, PACK], F32)
+        bw_bf = sb("bw_bf", [P, 2, PACK], BF16)
+        bw_f = sb("bw_f", [P, 2, PACK], F32)
+        pv = sb("pv", [P, P], BF16)
+        ident = sb("ident", [P, P], BF16)
+        pcol = sb("pcol", [P, 5, MT], F32)
+        half = sb("half", [P, MT], F32)
+        veps = sb("veps", [P, MT], F32)
+        rstd = sb("rstd", [P, MT], F32)
+        scale = sb("scale", [P, MT], F32)
+        dif = sb("dif", [P, MT], F32)
+        prod = sb("prod", [P, MT], F32)
+        shift = sb("shift", [P, MT], F32)
+        y_mid = sb("y_mid", [P, MT, P], F32)
+
+        nc.gpsimd.memset(ww_sraw[:].bitcast(I32), 0)
+        nc.gpsimd.memset(wf_s[:].rearrange("p g n -> p (g n)").bitcast(I32), 0)
+        nc.gpsimd.memset(pv[:], 0.0)
+        nc.gpsimd.memset(half[:], -0.5)
+        make_identity(nc, ident[:])
+
+        def load_ctx(b, lo, hi):
+            nc.sync.dma_start(
+                out=ctx_raw[b][:, :, lo:hi], in_=context[b].rearrange("(p t) h w -> p t (h w)", t=PACK)[:, :, lo:hi]
+            )
+
+        def load_hi(b, g):
+            nc.sync.dma_start(
+                out=hi_raw[b][g][:],
+                in_=high_feats_bytes[b].rearrange("(g p t) h w -> g p t (h w)", p=P, t=PACK)[g],
+            )
+
+        def load_wf(g):
+            nc.sync.dma_start(out=wf_q[g][:].bitcast(I32), in_=wf_words[g].bitcast(I32))
+
+        nc.scalar.dma_start(out=hs[:], in_=high_feats_scale[0, :, 0, 0].rearrange("(g p t) -> p g t", p=P, t=PACK))
+        nc.sync.dma_start(out=ww_raw[:].bitcast(I32), in_=ww_words[0].bitcast(I32))
+        load_hi(0, 0)
+        load_ctx(0, 0, 256)
+        for q in range(4):
+            nc.sync.dma_start(
+                out=ww_sraw[32 * q : 32 * q + 4, :].bitcast(I32), in_=ww_scales[0, 4 * q : 4 * q + 4, :].bitcast(I32)
+            )
+        for q in range(4):
+            nc.sync.dma_start(
+                out=wf_s[32 * q : 32 * q + 4, :, :].bitcast(I32),
+                in_=wf_scales[:, 4 * q : 4 * q + 4, :].bitcast(I32).rearrange("g q n -> q g n"),
+            )
+        nc.scalar.dma_start(out=bw_bf[:], in_=bw.rearrange("(h p t) -> p h t", h=2, t=PACK))
+        load_ctx(0, 256, NPIX)
+        load_wf(2)
+        load_hi(0, 1)
+        load_wf(0)
+        load_hi(0, 2)
+        load_wf(3)
+        load_wf(1)
+        load_hi(0, 3)
+        load_ctx(1, 0, NPIX)
+        for v, vec in enumerate((bfuse, gf, bef, mf, vf)):
+            nc.sync.dma_start(out=pv[v * MT : (v + 1) * MT, :], in_=vec.rearrange("(j p) -> j p", p=P))
+        load_wf(4)
+        load_wf(5)
+        for g in range(HG):
+            load_hi(1, g)
+
+        wide = {}
+        inter = {}
+
+        def widen(b, g, ts, engine):
+            if (b, g) not in wide:
+                wide[b, g] = wide_pool.tile([P, PACK, NPIX], BF16, name="wide_t", align_bytes=64)
+            for t in ts:
+                src = hi_raw[b][g][:, t, :].bitcast(FP8)
+                dst = wide[b, g][:, t, :]
+                if engine == "s":
+                    nc.scalar.activation(out=dst, in_=src, func=COPY, scale=hs[:, g, t : t + 1])
+                else:
+                    nc.vector.tensor_scalar(out=dst, in0=src, scalar1=hs[:, g, t : t + 1], scalar2=None, op0=MULT)
+
+        def widen_s(b, g):
+            widen(b, g, range(PACK), "s")
+
+        def interleave(b, g, engine):
+            if (b, g) not in inter:
+                inter[b, g] = inter_pool.tile([P, NPIX, PACK], BF16, name="inter_t", align_bytes=64)
+            cut = NPIX - SHARE[b]
+            lo, hi = (0, cut) if engine == "v" else (cut, NPIX)
+            if lo == hi:
+                return
+            src = wide[b, g][:, :, lo:hi].rearrange("p t n -> p n t")
+            dst = inter[b, g][:, lo:hi, :]
+            if engine == "v":
+                nc.vector.tensor_copy(out=dst, in_=src)
+            else:
+                nc.scalar.copy(out=dst, in_=src)
+
+        def quantize(codes, scales, src, at, lo, hi):
+            nc.vector.quantize_mx(
+                out=codes[:, at + lo : at + hi].bitcast(FP8X4),
+                scales=scales[:, at + lo : at + hi],
+                in_=src[:, lo:hi, :].rearrange("p n t -> p (n t)"),
+            )
+
+        def quantize_batch(codes, scales, src, b):
+            runs = ((0, 512), (512, NPIX)) if b == 0 else ((64, NPIX), (0, 64))
+            for lo, hi in runs:
+                quantize(codes, scales, src, NPIX * b, lo, hi)
+
+        def quantize_hi(b, g):
+            quantize_batch(kq[2 + g], ks[2 + g], inter[b, g], b)
+
+        def quantize_c(h, lo, hi):
+            quantize(kq[h], ks[h], c_int[h], 0, lo, hi)
+
+        quads = {}
+
+        def stage1(h, lo):
+            i = len(quads)
+            t_bank = bank(6 + i % 2, [P, PACK, P])
+            quads[h, lo] = t_bank
+            px = slice(lo, lo + P)
+            for t in range(PACK):
+                w = 512 * h + P * t
+                nc.tensor.matmul_mx(
+                    out=t_bank[:, t, :],
+                    lhsT=ww_q[:, 2 * w : 2 * w + 2 * P].bitcast(FP4X4),
+                    lhsT_scale=ww_s[:, w : w + P],
+                    rhs=ctx_q[:, px].bitcast(FP8X4),
+                    rhs_scale=ctx_s[:, px],
+                    start=True,
+                    stop=True,
+                )
+
+        def finish_c(h, lo):
+            nc.vector.tensor_tensor(
+                out=c_int[h][:, lo : lo + P, :],
+                in0=quads[h, lo][:].rearrange("p t n -> p n t"),
+                in1=bw_f[:, h, :].unsqueeze(1).to_broadcast([P, P, PACK]),
+                op=ADD,
+            )
+
+        def accumulate(dst, g, m, lo, hi, first, last):
+            nc.tensor.matmul_mx(
+                out=dst,
+                lhsT=wf_q[g][:, 2 * P * m : 2 * P * m + 2 * P].bitcast(FP4X4),
+                lhsT_scale=wf_s[:, g, P * m : P * m + P],
+                rhs=kq[g][:, lo:hi].bitcast(FP8X4),
+                rhs_scale=ks[g][:, lo:hi],
+                start=first,
+                stop=last,
+            )
+
+        def finish_y(dst, src, m, engine):
+            if engine == "s":
+                nc.scalar.activation(out=dst, in_=src, func=IDENT, scale=scale[:, m : m + 1], bias=shift[:, m : m + 1])
+            else:
+                nc.vector.tensor_scalar(
+                    out=dst, in0=src, scalar1=scale[:, m : m + 1], scalar2=shift[:, m : m + 1], op0=MULT, op1=ADD
+                )
+
+        def finish_wide(m, b, src, engine):
+            y = y_pool.tile([P, 512], F32, name="y_t")
+            finish_y(y[:], src, m, engine)
+            nc.sync.dma_start(
+                out=out[b].rearrange("(m p) h w -> m p (h w)", p=P)[m][:, 64 * b : 64 * b + 512], in_=y[:]
+            )
+
+        def permute_words(h):
+            nc.vector.tensor_copy(
+                out=ww_q[:, 1024 * h : 1024 * h + 1024].rearrange("p (t i e) -> p t i e", t=PACK, e=2),
+                in_=ww_raw[:, 1024 * h : 1024 * h + 1024].rearrange("p (i t e) -> p t i e", t=PACK, e=2),
+            )
+
+        def ctx_interleave(b, lo, hi, engine):
+            src = ctx_raw[b][:, :, lo:hi].rearrange("p t n -> p n t")
+            dst = ctx_int[b][:, lo:hi, :]
+            if engine == "v":
+                nc.vector.tensor_copy(out=dst, in_=src)
+            elif engine == "s":
+                nc.scalar.copy(out=dst, in_=src)
+            else:
+                nc.gpsimd.tensor_scalar(out=dst, in0=src, scalar1=1.0, scalar2=0.0, op0=MULT, op1=ADD)
+
+        def permute_scales(h):
+            nc.vector.tensor_copy(
+                out=ww_s[:, 512 * h : 512 * h + 512].rearrange("p (t i) -> p t i", t=PACK),
+                in_=ww_sraw[:, 512 * h : 512 * h + 512].rearrange("p (i t) -> p t i", t=PACK),
+            )
+
+        acc = {}
+        for m in range(6):
+            acc[m] = bank(m, [P, 512])
+
+        def acc_a(g, first=False, last=False):
+            for m in range(6):
+                accumulate(acc[m][:], g, m, 0, 512, first, last)
+
+        permute_words(0)
+        widen(0, 0, (0, 1, 2), "s")
+        widen(0, 0, (3,), "v")
+        ctx_interleave(0, 0, 256, "v")
+        permute_scales(0)
+        interleave(0, 0, "s")
+        quantize(ctx_q, ctx_s, ctx_int[0], 0, 0, 256)
+        interleave(0, 0, "v")
+        stage1(0, 0)
+        stage1(0, 128)
+        nc.vector.tensor_copy(out=bw_f[:], in_=bw_bf[:])
+        permute_scales(1)
+        quantize_hi(0, 0)
+        finish_c(0, 0)
+        ctx_interleave(0, 256, NPIX, "s")
+        acc_a(2, True)
+        finish_c(0, 128)
+        quantize(ctx_q, ctx_s, ctx_int[0], 0, 256, 512)
+        widen_s(0, 1)
+        stage1(0, 256)
+        stage1(0, 384)
+        permute_words(1)
+        finish_c(0, 256)
+        finish_c(0, 384)
+        interleave(0, 1, "s")
+        stage1(1, 0)
+        stage1(1, 128)
+        finish_c(1, 0)
+        quantize_c(0, 0, 512)
+        finish_c(1, 128)
+        stage1(1, 256)
+        acc_a(0)
+        interleave(0, 1, "v")
+        stage1(1, 384)
+        finish_c(1, 256)
+        quantize_hi(0, 1)
+        finish_c(1, 384)
+        acc_a(3)
+        ctx_interleave(1, 0, NPIX, "g")
+        widen_s(0, 2)
+        quantize(ctx_q, ctx_s, ctx_int[0], 0, 512, NPIX)
+        quantize_c(1, 0, 512)
+        acc_a(1)
+        interleave(0, 2, "s")
+        interleave(0, 2, "v")
+        quantize_batch(ctx_q, ctx_s, ctx_int[1], 1)
+        quantize_hi(0, 2)
+        pt = bank(6, [P, P], BF16)
+        nc.tensor.transpose(pt[:], pv[:], ident[:])
+        nc.vector.tensor_copy(out=pcol[:].rearrange("p v m -> p (v m)"), in_=pt[:, 0 : 5 * MT])
+        stage1(0, 640)
+        stage1(0, 768)
+        finish_c(0, 640)
+        nc.gpsimd.tensor_scalar(out=veps[:], in0=pcol[:, 4, :], scalar1=EPS, scalar2=None, op0=ADD)
+        nc.gpsimd.tensor_tensor(out=rstd[:], in0=veps[:], in1=half[:], op=POW)
+        nc.gpsimd.tensor_tensor(out=scale[:], in0=rstd[:], in1=pcol[:, 1, :], op=MULT)
+        nc.gpsimd.tensor_tensor(out=dif[:], in0=pcol[:, 0, :], in1=pcol[:, 3, :], op=SUB)
+        nc.gpsimd.tensor_tensor(out=prod[:], in0=dif[:], in1=scale[:], op=MULT)
+        nc.gpsimd.tensor_tensor(out=shift[:], in0=prod[:], in1=pcol[:, 2, :], op=ADD)
+        acc_a(4)
+        finish_c(0, 768)
+        stage1(0, 896)
+        stage1(0, 1024)
+        widen_s(0, 3)
+        interleave(0, 3, "s")
+        interleave(0, 3, "v")
+        finish_c(0, 896)
+        quantize_hi(0, 3)
+        stage1(1, 640)
+        acc_a(5, False, True)
+        widen_s(1, 0)
+        finish_c(0, 1024)
+        finish_c(1, 640)
+        stage1(1, 768)
+
+        def straight(m, i):
+            acc[m] = bank(i, [P, 512])
+            for g in range(KG):
+                accumulate(acc[m][:], g, m, 0, 512, g == 0, g == KG - 1)
+
+        finish_wide(0, 0, acc[0][:], "s")
+        finish_wide(1, 0, acc[1][:], "s")
+        quantize_c(0, 640, 1152)
+        straight(6, 0)
+        finish_c(1, 768)
+        stage1(1, 896)
+        stage1(1, 1024)
+        straight(7, 1)
+        for m in range(2, 6):
+            finish_wide(m, 0, acc[m][:], "s")
+        interleave(1, 0, "v")
+        finish_c(1, 896)
+        interleave(1, 0, "s")
+        widen_s(1, 1)
+        finish_c(1, 1024)
+        quantize_hi(1, 0)
+        stage1(0, 512)
+        stage1(1, 512)
+        finish_c(0, 512)
+        quantize_c(1, 640, 1152)
+        finish_c(1, 512)
+        finish_wide(6, 0, acc[6][:], "s")
+        finish_wide(7, 0, acc[7][:], "s")
+
+        for m, i in enumerate((2, 3, 4, 5, 0, 1, 6, 7)):
+            acc[m] = bank(i, [P, 512])
+
+        def acc_c(g, m, first=False, last=False):
+            accumulate(acc[m][:], g, m, 640, 1152, first, last)
+
+        for m in range(MT):
+            acc_c(0, m, True)
+        for m in range(MT):
+            acc_c(2, m)
+        for m in range(MT):
+            acc_c(1, m)
+        interleave(1, 1, "s")
+        widen_s(1, 2)
+        interleave(1, 1, "v")
+        quantize_c(0, 512, 640)
+        quantize_c(1, 512, 640)
+        quantize_hi(1, 1)
+        for m in range(MT):
+            acc_c(3, m)
+        interleave(1, 2, "s")
+        widen_s(1, 3)
+        interleave(1, 2, "v")
+        quantize_hi(1, 2)
+        interleave(1, 3, "s")
+        interleave(1, 3, "v")
+        quantize_hi(1, 3)
+        for m in range(MT):
+            acc_c(4, m)
+            acc_c(5, m, False, True)
+            finish_wide(m, 1, acc[m][:], "sv"[m % 2])
+        for i in range(2):
+            mid = bank((2, 3)[i], [P, 4, P])
+            for j in range(4):
+                m = 4 * i + j
+                for g in range(KG):
+                    accumulate(mid[:, j, :], g, m, 512, 640, g == 0, g == KG - 1)
+            for j in range(4):
+                m = 4 * i + j
+                finish_y(y_mid[:, m, :], mid[:, j, :], m, "sv"[j % 2])
+            ms = slice(4 * i, 4 * i + 4)
+            for b, lo in ((0, 512), (1, 0)):
+                nc.sync.dma_start(
+                    out=out[b].rearrange("(m p) h w -> p m (h w)", p=P)[:, ms, lo : lo + 64],
+                    in_=y_mid[:, ms, 64 * b : 64 * b + 64],
+                )

@@ -28,6 +28,7 @@ PACK = 4
 KG = CF // 512
 HG = CH // 512
 MT = CO // P
+WARM = 13
 SHARE = (256, 64)
 
 
@@ -242,10 +243,8 @@ def tile_afnb_pb_w4_kernel(
             dst = ctx_int[b][:, lo:hi, :]
             if engine == "v":
                 nc.vector.tensor_copy(out=dst, in_=src)
-            elif engine == "s":
-                nc.scalar.copy(out=dst, in_=src)
             else:
-                nc.gpsimd.tensor_scalar(out=dst, in0=src, scalar1=1.0, scalar2=0.0, op0=MULT, op1=ADD)
+                nc.scalar.copy(out=dst, in_=src)
 
         def permute_scales(h):
             nc.vector.tensor_copy(
@@ -254,13 +253,16 @@ def tile_afnb_pb_w4_kernel(
             )
 
         acc = {}
-        for m in range(6):
-            acc[m] = bank(m, [P, 512])
 
         def acc_a(g, first=False, last=False):
             for m in range(6):
                 accumulate(acc[m][:], g, m, 0, 512, first, last)
 
+        idle = sb("idle", [P, 512], BF16)
+        nc.vector.memset(idle[:], 0.0)
+        warm = bank(5, [P, 512])
+        for i in range(WARM):
+            nc.tensor.matmul(warm[:], lhsT=idle[:, 0:P], rhs=idle[:], start=True, stop=True)
         permute_words(0)
         widen(0, 0, (0, 1, 2), "s")
         widen(0, 0, (3,), "v")
@@ -276,6 +278,8 @@ def tile_afnb_pb_w4_kernel(
         quantize_hi(0, 0)
         finish_c(0, 0)
         ctx_interleave(0, 256, NPIX, "s")
+        for m in range(6):
+            acc[m] = bank(m, [P, 512])
         acc_a(2, True)
         finish_c(0, 128)
         quantize(ctx_q, ctx_s, ctx_int[0], 0, 256, 512)
@@ -299,11 +303,12 @@ def tile_afnb_pb_w4_kernel(
         quantize_hi(0, 1)
         finish_c(1, 384)
         acc_a(3)
-        ctx_interleave(1, 0, NPIX, "g")
         widen_s(0, 2)
         quantize(ctx_q, ctx_s, ctx_int[0], 0, 512, NPIX)
+        ctx_interleave(1, 0, 320, "v")
         quantize_c(1, 0, 512)
         acc_a(1)
+        ctx_interleave(1, 320, NPIX, "s")
         interleave(0, 2, "s")
         interleave(0, 2, "v")
         quantize_batch(ctx_q, ctx_s, ctx_int[1], 1)

from contextlib import ExitStack

import concourse.mybir as mybir
from concourse.masks import make_identity

B, CV, CH, CO, NPIX = 2, 512, 2048, 1024, 576
CF = CO + CH
EPS = 1e-5
FLOPS = 2 * B * NPIX * CO * (CV + CF)

F32 = mybir.dt.float32
BF16 = mybir.dt.bfloat16
U32 = mybir.dt.uint32
I32 = mybir.dt.int32
U8 = mybir.dt.uint8
FP8 = mybir.dt.float8_e4m3fn
FP8X4 = mybir.dt.float8_e4m3fn_x4
FP4X4 = mybir.dt.float4_e2m1fn_x4
ADD = mybir.AluOpType.add
SUB = mybir.AluOpType.subtract
MULT = mybir.AluOpType.mult
POW = mybir.AluOpType.pow
IDENT = mybir.ActivationFunctionType.Identity
COPY = mybir.ActivationFunctionType.Copy

P = 128
PACK = 4
KG = CF // 512
HG = CH // 512
MT = CO // P
WARM = 13
SHARE = (256, 64)


def tile_afnb_pb_w4_kernel(
    tc, context, high_feats_bytes, high_feats_scale, ww_words, ww_scales, bw, wf_words, wf_scales, bfuse, gf, bef, mf, vf, out
):
    nc = tc.nc
    with ExitStack() as ctx:
        keep = ctx.enter_context(tc.tile_pool(name="keep", bufs=1))
        wide_pool = ctx.enter_context(tc.tile_pool(name="wide", bufs=4))
        inter_pool = ctx.enter_context(tc.tile_pool(name="inter", bufs=3))
        y_pool = ctx.enter_context(tc.tile_pool(name="y", bufs=8))
        psum = ctx.enter_context(tc.psum_pool(name="psum", bufs=1))
        ctx.enter_context(tc.manual_schedule())

        def sb(name, shape, dt):
            return keep.tile(shape, dt, name=name, align_bytes=64)

        def bank(i, shape, dt=F32):
            return psum.tile(shape, dt, name="bank%d" % i)

        NALL = B * NPIX
        ctx_raw = [sb("ctx_raw%d" % b, [P, PACK, NPIX], BF16) for b in range(B)]
        ctx_int = [sb("ctx_int%d" % b, [P, NPIX, PACK], BF16) for b in range(B)]
        ctx_q = sb("ctx_q", [P, NALL], U32)
        ctx_s = sb("ctx_s", [P, NALL], U8)
        hi_raw = [[sb("hi_raw%d_%d" % (b, g), [P, PACK, NPIX], U8) for g in range(HG)] for b in range(B)]
        c_int = [sb("c_int%d" % h, [P, NALL, PACK], BF16) for h in range(2)]
        kq = [sb("kq%d" % g, [P, NALL], U32) for g in range(KG)]
        ks = [sb("ks%d" % g, [P, NALL], U8) for g in range(KG)]
        ww_raw = sb("ww_raw", [P, 2 * CO], U8)
        ww_q = sb("ww_q", [P, 2 * CO], U8)
        ww_sraw = sb("ww_sraw", [P, CO], U8)
        ww_s = sb("ww_s", [P, CO], U8)
        wf_q = [sb("wf_q%d" % g, [P, 2 * CO], U8) for g in range(KG)]
        wf_s = sb("wf_s", [P, KG, CO], U8)
        hs = sb("hs", [P, HG, PACK], F32)
        bw_bf = sb("bw_bf", [P, 2, PACK], BF16)
        bw_f = sb("bw_f", [P, 2, PACK], F32)
        pv = sb("pv", [P, P], BF16)
        ident = sb("ident", [P, P], BF16)
        pcol = sb("pcol", [P, 5, MT], F32)
        half = sb("half", [P, MT], F32)
        veps = sb("veps", [P, MT], F32)
        rstd = sb("rstd", [P, MT], F32)
        scale = sb("scale", [P, MT], F32)
        dif = sb("dif", [P, MT], F32)
        prod = sb("prod", [P, MT], F32)
        shift = sb("shift", [P, MT], F32)
        y_mid = sb("y_mid", [P, MT, P], F32)

        nc.gpsimd.memset(ww_sraw[:].bitcast(I32), 0)
        nc.gpsimd.memset(wf_s[:].rearrange("p g n -> p (g n)").bitcast(I32), 0)
        nc.gpsimd.memset(pv[:], 0.0)
        nc.gpsimd.memset(half[:], -0.5)
        make_identity(nc, ident[:])

        def load_ctx(b, lo, hi):
            nc.sync.dma_start(
                out=ctx_raw[b][:, :, lo:hi], in_=context[b].rearrange("(p t) h w -> p t (h w)", t=PACK)[:, :, lo:hi]
            )

        def load_hi(b, g):
            nc.sync.dma_start(
                out=hi_raw[b][g][:],
                in_=high_feats_bytes[b].rearrange("(g p t) h w -> g p t (h w)", p=P, t=PACK)[g],
            )

        def load_wf(g):
            nc.sync.dma_start(out=wf_q[g][:].bitcast(I32), in_=wf_words[g].bitcast(I32))

        nc.scalar.dma_start(out=hs[:], in_=high_feats_scale[0, :, 0, 0].rearrange("(g p t) -> p g t", p=P, t=PACK))
        nc.sync.dma_start(out=ww_raw[:].bitcast(I32), in_=ww_words[0].bitcast(I32))
        load_hi(0, 0)
        load_ctx(0, 0, 256)
        for q in range(4):
            nc.sync.dma_start(
                out=ww_sraw[32 * q : 32 * q + 4, :].bitcast(I32), in_=ww_scales[0, 4 * q : 4 * q + 4, :].bitcast(I32)
            )
        for q in range(4):
            nc.sync.dma_start(
                out=wf_s[32 * q : 32 * q + 4, :, :].bitcast(I32),
                in_=wf_scales[:, 4 * q : 4 * q + 4, :].bitcast(I32).rearrange("g q n -> q g n"),
            )
        nc.scalar.dma_start(out=bw_bf[:], in_=bw.rearrange("(h p t) -> p h t", h=2, t=PACK))
        load_ctx(0, 256, NPIX)
        load_wf(2)
        load_hi(0, 1)
        load_wf(0)
        load_hi(0, 2)
        load_wf(3)
        load_wf(1)
        load_hi(0, 3)
        load_ctx(1, 0, NPIX)
        for v, vec in enumerate((bfuse, gf, bef, mf, vf)):
            nc.sync.dma_start(out=pv[v * MT : (v + 1) * MT, :], in_=vec.rearrange("(j p) -> j p", p=P))
        load_wf(4)
        load_wf(5)
        for g in range(HG):
            load_hi(1, g)

        wide = {}
        inter = {}

        def widen(b, g, ts, engine):
            if (b, g) not in wide:
                wide[b, g] = wide_pool.tile([P, PACK, NPIX], BF16, name="wide_t", align_bytes=64)
            for t in ts:
                src = hi_raw[b][g][:, t, :].bitcast(FP8)
                dst = wide[b, g][:, t, :]
                if engine == "s":
                    nc.scalar.activation(out=dst, in_=src, func=COPY, scale=hs[:, g, t : t + 1])
                else:
                    nc.vector.tensor_scalar(out=dst, in0=src, scalar1=hs[:, g, t : t + 1], scalar2=None, op0=MULT)

        def widen_s(b, g):
            widen(b, g, range(PACK), "s")

        def interleave(b, g, engine):
            if (b, g) not in inter:
                inter[b, g] = inter_pool.tile([P, NPIX, PACK], BF16, name="inter_t", align_bytes=64)
            cut = NPIX - SHARE[b]
            lo, hi = (0, cut) if engine == "v" else (cut, NPIX)
            if lo == hi:
                return
            src = wide[b, g][:, :, lo:hi].rearrange("p t n -> p n t")
            dst = inter[b, g][:, lo:hi, :]
            if engine == "v":
                nc.vector.tensor_copy(out=dst, in_=src)
            else:
                nc.scalar.copy(out=dst, in_=src)

        def quantize(codes, scales, src, at, lo, hi):
            nc.vector.quantize_mx(
                out=codes[:, at + lo : at + hi].bitcast(FP8X4),
                scales=scales[:, at + lo : at + hi],
                in_=src[:, lo:hi, :].rearrange("p n t -> p (n t)"),
            )

        def quantize_batch(codes, scales, src, b):
            runs = ((0, 512), (512, NPIX)) if b == 0 else ((64, NPIX), (0, 64))
            for lo, hi in runs:
                quantize(codes, scales, src, NPIX * b, lo, hi)

        def quantize_hi(b, g):
            quantize_batch(kq[2 + g], ks[2 + g], inter[b, g], b)

        def quantize_c(h, lo, hi):
            quantize(kq[h], ks[h], c_int[h], 0, lo, hi)

        quads = {}

        def stage1(h, lo):
            i = len(quads)
            t_bank = bank(6 + i % 2, [P, PACK, P])
            quads[h, lo] = t_bank
            px = slice(lo, lo + P)
            for t in range(PACK):
                w = 512 * h + P * t
                nc.tensor.matmul_mx(
                    out=t_bank[:, t, :],
                    lhsT=ww_q[:, 2 * w : 2 * w + 2 * P].bitcast(FP4X4),
                    lhsT_scale=ww_s[:, w : w + P],
                    rhs=ctx_q[:, px].bitcast(FP8X4),
                    rhs_scale=ctx_s[:, px],
                    start=True,
                    stop=True,
                )

        def finish_c(h, lo):
            nc.vector.tensor_tensor(
                out=c_int[h][:, lo : lo + P, :],
                in0=quads[h, lo][:].rearrange("p t n -> p n t"),
                in1=bw_f[:, h, :].unsqueeze(1).to_broadcast([P, P, PACK]),
                op=ADD,
            )

        def accumulate(dst, g, m, lo, hi, first, last):
            nc.tensor.matmul_mx(
                out=dst,
                lhsT=wf_q[g][:, 2 * P * m : 2 * P * m + 2 * P].bitcast(FP4X4),
                lhsT_scale=wf_s[:, g, P * m : P * m + P],
                rhs=kq[g][:, lo:hi].bitcast(FP8X4),
                rhs_scale=ks[g][:, lo:hi],
                start=first,
                stop=last,
            )

        def finish_y(dst, src, m, engine):
            if engine == "s":
                nc.scalar.activation(out=dst, in_=src, func=IDENT, scale=scale[:, m : m + 1], bias=shift[:, m : m + 1])
            else:
                nc.vector.tensor_scalar(
                    out=dst, in0=src, scalar1=scale[:, m : m + 1], scalar2=shift[:, m : m + 1], op0=MULT, op1=ADD
                )

        def finish_wide(m, b, src, engine):
            y = y_pool.tile([P, 512], F32, name="y_t")
            finish_y(y[:], src, m, engine)
            nc.sync.dma_start(
                out=out[b].rearrange("(m p) h w -> m p (h w)", p=P)[m][:, 64 * b : 64 * b + 512], in_=y[:]
            )

        def permute_words(h):
            nc.vector.tensor_copy(
                out=ww_q[:, 1024 * h : 1024 * h + 1024].rearrange("p (t i e) -> p t i e", t=PACK, e=2),
                in_=ww_raw[:, 1024 * h : 1024 * h + 1024].rearrange("p (i t e) -> p t i e", t=PACK, e=2),
            )

        def ctx_interleave(b, lo, hi, engine):
            src = ctx_raw[b][:, :, lo:hi].rearrange("p t n -> p n t")
            dst = ctx_int[b][:, lo:hi, :]
            if engine == "v":
                nc.vector.tensor_copy(out=dst, in_=src)
            else:
                nc.scalar.copy(out=dst, in_=src)

        def permute_scales(h):
            nc.vector.tensor_copy(
                out=ww_s[:, 512 * h : 512 * h + 512].rearrange("p (t i) -> p t i", t=PACK),
                in_=ww_sraw[:, 512 * h : 512 * h + 512].rearrange("p (i t) -> p t i", t=PACK),
            )

        acc = {}

        def acc_a(g, first=False, last=False):
            for m in range(6):
                accumulate(acc[m][:], g, m, 0, 512, first, last)

        idle = sb("idle", [P, 512], BF16)
        nc.vector.memset(idle[:], 0.0)
        warm = bank(5, [P, 512])
        for i in range(WARM):
            nc.tensor.matmul(warm[:], lhsT=idle[:, 0:P], rhs=idle[:], start=True, stop=True)
        permute_words(0)
        widen(0, 0, (0, 1, 2), "s")
        widen(0, 0, (3,), "v")
        ctx_interleave(0, 0, 256, "v")
        permute_scales(0)
        interleave(0, 0, "s")
        quantize(ctx_q, ctx_s, ctx_int[0], 0, 0, 256)
        interleave(0, 0, "v")
        stage1(0, 0)
        stage1(0, 128)
        nc.vector.tensor_copy(out=bw_f[:], in_=bw_bf[:])
        permute_scales(1)
        quantize_hi(0, 0)
        finish_c(0, 0)
        ctx_interleave(0, 256, NPIX, "s")
        for m in range(6):
            acc[m] = bank(m, [P, 512])
        acc_a(2, True)
        finish_c(0, 128)
        quantize(ctx_q, ctx_s, ctx_int[0], 0, 256, 512)
        widen_s(0, 1)
        stage1(0, 256)
        stage1(0, 384)
        permute_words(1)
        finish_c(0, 256)
        finish_c(0, 384)
        interleave(0, 1, "s")
        stage1(1, 0)
        stage1(1, 128)
        finish_c(1, 0)
        quantize_c(0, 0, 512)
        finish_c(1, 128)
        stage1(1, 256)
        acc_a(0)
        interleave(0, 1, "v")
        stage1(1, 384)
        finish_c(1, 256)
        quantize_hi(0, 1)
        finish_c(1, 384)
        acc_a(3)
        widen_s(0, 2)
        quantize(ctx_q, ctx_s, ctx_int[0], 0, 512, NPIX)
        ctx_interleave(1, 0, 320, "v")
        quantize_c(1, 0, 512)
        acc_a(1)
        ctx_interleave(1, 320, NPIX, "s")
        interleave(0, 2, "s")
        interleave(0, 2, "v")
        quantize_batch(ctx_q, ctx_s, ctx_int[1], 1)
        quantize_hi(0, 2)
        pt = bank(6, [P, P], BF16)
        nc.tensor.transpose(pt[:], pv[:], ident[:])
        nc.vector.tensor_copy(out=pcol[:].rearrange("p v m -> p (v m)"), in_=pt[:, 0 : 5 * MT])
        stage1(0, 640)
        stage1(0, 768)
        finish_c(0, 640)
        nc.gpsimd.tensor_scalar(out=veps[:], in0=pcol[:, 4, :], scalar1=EPS, scalar2=None, op0=ADD)
        nc.gpsimd.tensor_tensor(out=rstd[:], in0=veps[:], in1=half[:], op=POW)
        nc.gpsimd.tensor_tensor(out=scale[:], in0=rstd[:], in1=pcol[:, 1, :], op=MULT)
        nc.gpsimd.tensor_tensor(out=dif[:], in0=pcol[:, 0, :], in1=pcol[:, 3, :], op=SUB)
        nc.gpsimd.tensor_tensor(out=prod[:], in0=dif[:], in1=scale[:], op=MULT)
        nc.gpsimd.tensor_tensor(out=shift[:], in0=prod[:], in1=pcol[:, 2, :], op=ADD)
        acc_a(4)
        finish_c(0, 768)
        stage1(0, 896)
        stage1(0, 1024)
        widen_s(0, 3)
        interleave(0, 3, "s")
        interleave(0, 3, "v")
        finish_c(0, 896)
        quantize_hi(0, 3)
        stage1(1, 640)
        acc_a(5, False, True)
        widen_s(1, 0)
        finish_c(0, 1024)
        finish_c(1, 640)
        stage1(1, 768)

        def straight(m, i):
            acc[m] = bank(i, [P, 512])
            for g in range(KG):
                accumulate(acc[m][:], g, m, 0, 512, g == 0, g == KG - 1)

        finish_wide(0, 0, acc[0][:], "s")
        finish_wide(1, 0, acc[1][:], "s")
        quantize_c(0, 640, 1152)
        straight(6, 0)
        finish_c(1, 768)
        stage1(1, 896)
        stage1(1, 1024)
        straight(7, 1)
        for m in range(2, 6):
            finish_wide(m, 0, acc[m][:], "s")
        interleave(1, 0, "v")
        finish_c(1, 896)
        interleave(1, 0, "s")
        widen_s(1, 1)
        finish_c(1, 1024)
        quantize_hi(1, 0)
        stage1(0, 512)
        stage1(1, 512)
        finish_c(0, 512)
        quantize_c(1, 640, 1152)
        finish_c(1, 512)
        finish_wide(6, 0, acc[6][:], "s")
        finish_wide(7, 0, acc[7][:], "s")

        for m, i in enumerate((2, 3, 4, 5, 0, 1, 6, 7)):
            acc[m] = bank(i, [P, 512])

        def acc_c(g, m, first=False, last=False):
            accumulate(acc[m][:], g, m, 640, 1152, first, last)

        for m in range(MT):
            acc_c(0, m, True)
        for m in range(MT):
            acc_c(2, m)
        for m in range(MT):
            acc_c(1, m)
        interleave(1, 1, "s")
        widen_s(1, 2)
        interleave(1, 1, "v")
        quantize_c(0, 512, 640)
        quantize_c(1, 512, 640)
        quantize_hi(1, 1)
        for m in range(MT):
            acc_c(3, m)
        interleave(1, 2, "s")
        widen_s(1, 3)
        interleave(1, 2, "v")
        quantize_hi(1, 2)
        interleave(1, 3, "s")
        interleave(1, 3, "v")
        quantize_hi(1, 3)
        for m in range(MT):
            acc_c(4, m)
            acc_c(5, m, False, True)
            finish_wide(m, 1, acc[m][:], "sv"[m % 2])
        for i in range(2):
            mid = bank((2, 3)[i], [P, 4, P])
            for j in range(4):
                m = 4 * i + j
                for g in range(KG):
                    accumulate(mid[:, j, :], g, m, 512, 640, g == 0, g == KG - 1)
            for j in range(4):
                m = 4 * i + j
                finish_y(y_mid[:, m, :], mid[:, j, :], m, "sv"[j % 2])
            ms = slice(4 * i, 4 * i + 4)
            for b, lo in ((0, 512), (1, 0)):
                nc.sync.dma_start(
                    out=out[b].rearrange("(m p) h w -> p m (h w)", p=P)[:, ms, lo : lo + 64],
                    in_=y_mid[:, ms, 64 * b : 64 * b + 64],
                )
